import numpy as np
import ml_dtypes


def mxq(x, axis, fmt="e4m3"):
    dtype, down = {"e4m3": (ml_dtypes.float8_e4m3fn, 7), "e5m2": (ml_dtypes.float8_e5m2, 14)}[fmt]
    v = np.moveaxis(np.asarray(x, np.float32).astype(ml_dtypes.bfloat16).astype(np.float64), axis, -1)
    blocks = v.reshape(v.shape[:-1] + (-1, 32))
    amax = np.abs(blocks).max(-1, keepdims=True)
    byte = np.maximum(np.where(amax > 0, np.frexp(amax)[1] - 1 + 127, 0) - down, 1)
    scale = np.exp2(byte - 127.0)
    codes = (blocks / scale).astype(np.float32).astype(dtype).astype(np.float64)
    return np.moveaxis((codes * scale).reshape(v.shape), -1, axis)


WIDE = False


def mx_kscale(k):
    if not WIDE:
        return np.ones(k)
    levels = np.array([10, -10, 5, -5, 0])
    if k % 512:
        return np.exp2(np.random.permutation(np.resize(levels, k // 32))).repeat(32)
    a = np.empty((k // 512, 16))
    for p in range(k // 512):
        a[p, :8] = np.random.permutation(np.resize(levels, 8))
        for g in range(8):
            far = levels[np.abs(levels - a[p, g]) >= 10]
            a[p, g + 8] = far[np.random.randint(len(far))]
    return np.exp2(a.ravel()).repeat(32)


BF16 = ml_dtypes.bfloat16


def bf(x):
    return np.asarray(x, np.float32).astype(BF16)


def f64(x):
    return np.asarray(x).astype(np.float64)


B, HH, WW, C, NH, KD, WS, SS = 4, 64, 64, 128, 8, 64, 8, 4
GH, GW, T, F = HH // WS, WW // WS, WS * WS, NH * KD
N = B * GH * GW


def setup_inputs():
    s = mx_kscale(F).reshape(NH, KD)
    return {"attn_ctx": bf(np.random.standard_normal((N, T, NH, KD)) * 0.4 * s),
            "x": bf(np.random.standard_normal((B, HH, WW, C))),
            "wo": bf(np.random.standard_normal((NH, KD, C)) * 2.0 / np.sqrt(F) / s[:, :, None]),
            "bo": bf(np.random.standard_normal(C) * 0.3)}


def reference(attn_ctx, x, wo, bo):
    o = f64(attn_ctx).reshape(N * T, F)
    proj = (mxq(o, 1, "e4m3") @ mxq(f64(wo).reshape(F, C), 0, "e4m3")) + f64(bo)
    merged = proj.reshape(B, GH, GW, WS, WS, C).swapaxes(2, 3).reshape(B, HH, WW, C)
    merged = np.roll(merged, shift=(SS, SS), axis=(1, 2))
    return f64(x) + merged

@@ -1,0 +1,226 @@
+from contextlib import ExitStack
+
+import concourse.mybir as mybir
+from concourse.masks import make_identity
+
+F32 = mybir.dt.float32
+BF16 = mybir.dt.bfloat16
+U32 = mybir.dt.uint32
+U8 = mybir.dt.uint8
+FP8X4 = mybir.dt.float8_e4m3fn_x4
+ADD = mybir.AluOpType.add
+
+P = 128
+FLOPS = 2 * 16384 * 512 * 128
+
+N_CHUNKS = 16
+N_UNITS = 2 * N_CHUNKS
+ATTN_BUFS = 6
+OUT_BUFS = 8
+OWN = 96
+
+
+def tile_windowattentionblock_pb_t_kernel(tc, attn_ctx, x, wo, bo, out):
+    nc = tc.nc
+    attn_v = attn_ctx.rearrange("n (ti tj) h d -> (n ti) (tj h d)", tj=8)
+    x_v = x.rearrange("b i (s r) c -> (b i s) (r c)", r=8)
+    out_v = out.rearrange("b i (s r) c -> (b i s) (r c)", r=8)
+    wo_v = wo.rearrange("h d c -> (h d) c").rearrange("(q t) c -> q (t c)", t=4)
+
+    with ExitStack() as ctx:
+        const = ctx.enter_context(tc.tile_pool(name="const", bufs=1))
+        attn_pool = ctx.enter_context(tc.tile_pool(name="attn", bufs=ATTN_BUFS))
+        grp_pool = ctx.enter_context(tc.tile_pool(name="grp", bufs=6))
+        grp0_pool = ctx.enter_context(tc.tile_pool(name="grp0", bufs=4))
+        code_pool = ctx.enter_context(tc.tile_pool(name="code", bufs=5))
+        out_pool = ctx.enter_context(tc.tile_pool(name="outp", bufs=OUT_BUFS))
+        tp_pool = ctx.enter_context(tc.psum_pool(name="tp", bufs=4))
+        mx_pool = ctx.enter_context(tc.psum_pool(name="mx", bufs=4))
+        ctx.enter_context(tc.manual_schedule())
+
+        attn_tiles = {}
+        x_tiles = {}
+        state = {}
+
+        def load_x(b):
+            nc.sync.dma_start(
+                out=x_tiles[b][:],
+                in_=x_v[b * 4 * P : (b + 1) * 4 * P, :].rearrange("(t q) f -> q t f", q=P),
+            )
+
+        def load_attn(c, pieces=1):
+            a_sb = attn_pool.tile([P, 4096], BF16, name="a_sb")
+            w = 4096 // pieces
+            for i in range(pieces):
+                nc.sync.dma_start(
+                    out=a_sb[:, i * w : (i + 1) * w],
+                    in_=attn_v[c * P : (c + 1) * P, i * w : (i + 1) * w],
+                )
+                if c == 0 and i == 0:
+                    nc.sync.dma_start(
+                        out=w_raw[:].rearrange("p t c -> p (t c)"), in_=wo_v
+                    )
+                    nc.sync.dma_start(out=brow[0:1, 0:P], in_=bo.unsqueeze(0))
+            attn_tiles[c] = a_sb
+
+        def load_chunk(c):
+            if c % 4 == 1:
+                load_x(c // 4)
+            load_attn(c)
+
+        brow = const.tile([P, 256], BF16, name="brow")
+        ones = const.tile([P, P], BF16, name="ones")
+        nc.vector.memset(brow[:], 0.0)
+        nc.vector.memset(ones[:], 1.0)
+        ident = const.tile([P, P], F32, name="ident")
+        make_identity(nc, ident[:])
+        for b in range(4):
+            x_tiles[b] = const.tile([P, 4, 1024], BF16, name="x_sb%d" % b)
+
+        w_raw = const.tile([P, 4, P], BF16, name="w_raw")
+        load_attn(0, pieces=2)
+        for c in range(1, ATTN_BUFS):
+            load_chunk(c)
+
+        id_v = ident[:].rearrange("p (g j t) -> p g t j", g=2, j=8)
+        perm_a = const.tile([P, 2, 8, 8], F32, name="perm_a")
+        perm_b = const.tile([P, 2, 8, 8], F32, name="perm_b")
+        nc.vector.tensor_copy(out=perm_a[:], in_=id_v)
+        nc.vector.tensor_copy(out=perm_b[:, :, :, 1:8], in_=id_v[:, :, :, 0:7])
+        nc.vector.tensor_copy(out=perm_b[:, :, :, 0:1], in_=id_v[:, :, :, 7:8])
+        perms = [
+            perm_a[:].rearrange("p g t s -> p (g t s)"),
+            perm_b[:].rearrange("p g t s -> p (g t s)"),
+        ]
+
+        bias_bc = const.tile([P, P], F32, name="bias_bc")
+
+        def spread_bias():
+            bias_ps = mx_pool.tile([P, 4, P], F32, name="bias_ps", tag="mx")
+            nc.tensor.matmul(
+                out=bias_ps[:, 0:2, :].rearrange("p a c -> p (a c)"),
+                lhsT=ones[:],
+                rhs=brow[:],
+                start=True,
+                stop=True,
+            )
+            nc.vector.tensor_copy(out=bias_bc[:], in_=bias_ps[:, 0, :])
+
+        w_grp = const.tile([P, P, 4], BF16, name="w_grp", align_bytes=64)
+        nc.vector.tensor_copy(out=w_grp[:], in_=w_raw[:].rearrange("p t c -> p c t"))
+        w_codes = const.tile([P, P], U32, name="w_codes", align_bytes=64)
+        w_scales = const.tile([P, P], U8, name="w_scales", align_bytes=64)
+        nc.vector.quantize_mx(
+            out=w_codes[:].bitcast(FP8X4),
+            scales=w_scales[:],
+            in_=w_grp[:].rearrange("p c t -> p (c t)"),
+        )
+
+        def grp_of(t, half):
+            key = ("grp", t, half)
+            if key not in state:
+                if t % 4 == 0:
+                    state[key] = grp0_pool.tile([P, 2048], BF16, name="grp0", align_bytes=64)
+                else:
+                    state[key] = grp_pool.tile([P, 2048], BF16, name="grp", align_bytes=64)
+            return state[key]
+
+        def transpose_and_exit(u):
+            c, half = u // 2, u % 2
+            a32 = attn_tiles[c][:].bitcast(F32)
+            t_next = (c // 4) * 4 + (c + 1) % 4
+            own32 = grp_of(c, half)[:].bitcast(F32).rearrange("p (j m h) -> p j m h", j=4, h=2)
+            next32 = grp_of(t_next, half)[:].bitcast(F32).rearrange("p (j m h) -> p j m h", j=4, h=2)
+            banks = []
+            for b in range(2):
+                tp = tp_pool.tile([P, 2, 2, P], F32, name="tp")
+                for a in range(2):
+                    tj = half * 4 + b * 2 + a
+                    for h in range(2):
+                        words = slice(tj * 256 + h, (tj + 1) * 256, 2)
+                        nc.tensor.transpose(tp[:, a, h, :], a32[:, words], perms[half])
+                banks.append(tp)
+            for b in range(2):
+                src = banks[b][:].rearrange("p a h m -> p a m h")
+                nc.scalar.copy(out=own32[:, 2 * b : 2 * b + 2, P - OWN : P, :], in_=src[:, :, 0:OWN, :])
+                nc.scalar.copy(out=next32[:, 2 * b : 2 * b + 2, 0 : P - OWN, :], in_=src[:, :, OWN:P, :])
+
+        def quantise(t, half):
+            codes = code_pool.tile([P, 512], U32, name="codes", align_bytes=64)
+            scales = code_pool.tile([P, 512], U8, name="scales", align_bytes=64)
+            nc.vector.quantize_mx(
+                out=codes[:].bitcast(FP8X4), scales=scales[:], in_=state[("grp", t, half)][:]
+            )
+            state[("codes", t, half)] = (codes, scales)
+
+        def multiply(t, half):
+            codes, scales = state[("codes", t, half)]
+            mx = mx_pool.tile([P, 4, P], F32, name="mx")
+            for a in range(4):
+                cols = slice(a * P, (a + 1) * P)
+                nc.tensor.matmul_mx(
+                    out=mx[:, a, :],
+                    lhsT=codes[:, cols].bitcast(FP8X4),
+                    lhsT_scale=scales[:, cols],
+                    rhs=w_codes[:].bitcast(FP8X4),
+                    rhs_scale=w_scales[:],
+                    start=True,
+                    stop=True,
+                )
+            state[("mx", t, half)] = mx
+
+        def o_half(half):
+            lo = 512 if half == 0 else 0
+            return slice(lo, lo + 512)
+
+        def add_bias(t, half):
+            if half == 0:
+                state[("o", t)] = out_pool.tile([P, 1024], F32, name="o_sb")
+            nc.vector.tensor_tensor(
+                out=state[("o", t)][:, o_half(half)].rearrange("p (r c) -> p r c", r=4),
+                in0=x_tiles[t // 4][:, t % 4, o_half(half)].rearrange("p (r c) -> p r c", r=4),
+                in1=bias_bc[:].unsqueeze(1).to_broadcast([P, 4, P]),
+                op=ADD,
+            )
+
+        def add_product(t, half):
+            o_part = state[("o", t)][:, o_half(half)]
+            nc.vector.tensor_tensor(
+                out=o_part,
+                in0=state[("mx", t, half)][:].rearrange("p a c -> p (a c)"),
+                in1=o_part,
+                op=ADD,
+            )
+            if half == 1:
+                nc.sync.dma_start(out=out_v[t * P : (t + 1) * P, :], in_=state[("o", t)][:])
+
+        def complete_after(u):
+            c, half = u // 2, u % 2
+            done = []
+            if c % 4 != 0:
+                done.append((c, half))
+            elif c > 0:
+                done.append((c - 4, half))
+            if c == N_CHUNKS - 1:
+                done.append((c - 3, half))
+            return done
+
+        for s in range(N_UNITS + 3):
+            if s < N_UNITS:
+                transpose_and_exit(s)
+            if s == 1:
+                spread_bias()
+            if 0 <= s - 1 < N_UNITS:
+                for t, half in complete_after(s - 1):
+                    quantise(t, half)
+                    add_bias(t, half)
+            if 0 <= s - 2 < N_UNITS:
+                for t, half in complete_after(s - 2):
+                    multiply(t, half)
+            if s < N_UNITS and s % 2 == 1:
+                c_next = s // 2 + ATTN_BUFS
+                if c_next < N_CHUNKS:
+                    load_chunk(c_next)
+            if 0 <= s - 3 < N_UNITS:
+                for t, half in complete_after(s - 3):
+                    add_product(t, half)

@@ -14,10 +14,15 @@ P = 128
 FLOPS = 2 * 16384 * 512 * 128
 
 N_CHUNKS = 16
-N_UNITS = 2 * N_CHUNKS
 ATTN_BUFS = 6
-OUT_BUFS = 8
-OWN = 96
+OUT_BUFS = 16
+LAST_ROWS = 96
+
+ORDER = (
+    [c for c in range(N_CHUNKS // 2) if c % 4 != 3]
+    + [c for c in range(N_CHUNKS) if c % 4 == 3]
+    + [c for c in range(N_CHUNKS // 2, N_CHUNKS) if c % 4 != 3]
+)
 
 
 def tile_windowattentionblock_pb_t_kernel(tc, attn_ctx, x, wo, bo, out):
@@ -31,7 +36,7 @@ def tile_windowattentionblock_pb_t_kernel(tc, attn_ctx, x, wo, bo, out):
         const = ctx.enter_context(tc.tile_pool(name="const", bufs=1))
         attn_pool = ctx.enter_context(tc.tile_pool(name="attn", bufs=ATTN_BUFS))
         grp_pool = ctx.enter_context(tc.tile_pool(name="grp", bufs=6))
-        grp0_pool = ctx.enter_context(tc.tile_pool(name="grp0", bufs=4))
+        edge_pool = ctx.enter_context(tc.tile_pool(name="edge", bufs=8))
         code_pool = ctx.enter_context(tc.tile_pool(name="code", bufs=5))
         out_pool = ctx.enter_context(tc.tile_pool(name="outp", bufs=OUT_BUFS))
         tp_pool = ctx.enter_context(tc.psum_pool(name="tp", bufs=4))
@@ -39,49 +44,53 @@ def tile_windowattentionblock_pb_t_kernel(tc, attn_ctx, x, wo, bo, out):
         ctx.enter_context(tc.manual_schedule())
 
         attn_tiles = {}
-        x_tiles = {}
         state = {}
 
-        def load_x(b):
-            nc.sync.dma_start(
-                out=x_tiles[b][:],
-                in_=x_v[b * 4 * P : (b + 1) * 4 * P, :].rearrange("(t q) f -> q t f", q=P),
-            )
-
-        def load_attn(c, pieces=1):
-            a_sb = attn_pool.tile([P, 4096], BF16, name="a_sb")
-            w = 4096 // pieces
-            for i in range(pieces):
-                nc.sync.dma_start(
-                    out=a_sb[:, i * w : (i + 1) * w],
-                    in_=attn_v[c * P : (c + 1) * P, i * w : (i + 1) * w],
-                )
-                if c == 0 and i == 0:
-                    nc.sync.dma_start(
-                        out=w_raw[:].rearrange("p t c -> p (t c)"), in_=wo_v
-                    )
-                    nc.sync.dma_start(out=brow[0:1, 0:P], in_=bo.unsqueeze(0))
-            attn_tiles[c] = a_sb
-
-        def load_chunk(c):
-            if c % 4 == 1:
-                load_x(c // 4)
-            load_attn(c)
-
+        x_sb = const.tile([P, N_CHUNKS, 1024], BF16, name="x_sb")
+        w_raw = const.tile([P, 4, P], BF16, name="w_raw")
         brow = const.tile([P, 256], BF16, name="brow")
         ones = const.tile([P, P], BF16, name="ones")
+
+        def slots(t):
+            if t < N_CHUNKS - 1:
+                return [(0, P, t * P + 32)]
+            return [(0, LAST_ROWS, t * P + 32), (LAST_ROWS, P, 0)]
+
+        def load_x(t0, t1):
+            if t1 <= N_CHUNKS - 1:
+                nc.sync.dma_start(
+                    out=x_sb[:, t0:t1, :],
+                    in_=x_v[t0 * P + 32 : t1 * P + 32, :].rearrange("(t q) f -> q t f", q=P),
+                )
+            else:
+                for p0, p1, row in slots(t0):
+                    nc.sync.dma_start(out=x_sb[p0:p1, t0, :], in_=x_v[row : row + p1 - p0, :])
+
+        def load_attn(c, lo=0, hi=4096):
+            if c not in attn_tiles:
+                attn_tiles[c] = attn_pool.tile([P, 4096], BF16, name="a_sb")
+            nc.sync.dma_start(out=attn_tiles[c][:, lo:hi], in_=attn_v[c * P : (c + 1) * P, lo:hi])
+
+        x_before = {1: (1, 3), 2: (3, 7), 4: (7, 12), 7: (12, 15), 8: (15, 16)}
+
+        def load_step(i):
+            if i in x_before:
+                load_x(*x_before[i])
+            load_attn(ORDER[i])
+
         nc.vector.memset(brow[:], 0.0)
         nc.vector.memset(ones[:], 1.0)
+        load_attn(ORDER[0], 0, 1024)
+        nc.sync.dma_start(out=brow[0:1, 0:P], in_=bo.unsqueeze(0))
+        load_attn(ORDER[0], 1024, 2048)
+        nc.sync.dma_start(out=w_raw[:].rearrange("p t c -> p (t c)"), in_=wo_v)
+        load_x(0, 1)
+        load_attn(ORDER[0], 2048, 4096)
+        for i in range(1, ATTN_BUFS):
+            load_step(i)
+
         ident = const.tile([P, P], F32, name="ident")
         make_identity(nc, ident[:])
-        for b in range(4):
-            x_tiles[b] = const.tile([P, 4, 1024], BF16, name="x_sb%d" % b)
-
-        w_raw = const.tile([P, 4, P], BF16, name="w_raw")
-        load_attn(0, pieces=2)
-        for c in range(1, ATTN_BUFS):
-            load_chunk(c)
-
         id_v = ident[:].rearrange("p (g j t) -> p g t j", g=2, j=8)
         perm_a = const.tile([P, 2, 8, 8], F32, name="perm_a")
         perm_b = const.tile([P, 2, 8, 8], F32, name="perm_b")
@@ -94,6 +103,9 @@ def tile_windowattentionblock_pb_t_kernel(tc, attn_ctx, x, wo, bo, out):
         ]
 
         bias_bc = const.tile([P, P], F32, name="bias_bc")
+        w_grp = const.tile([P, P, 4], BF16, name="w_grp", align_bytes=64)
+        w_codes = const.tile([P, P], U32, name="w_codes", align_bytes=64)
+        w_scales = const.tile([P, P], U8, name="w_scales", align_bytes=64)
 
         def spread_bias():
             bias_ps = mx_pool.tile([P, 4, P], F32, name="bias_ps", tag="mx")
@@ -106,31 +118,25 @@ def tile_windowattentionblock_pb_t_kernel(tc, attn_ctx, x, wo, bo, out):
             )
             nc.vector.tensor_copy(out=bias_bc[:], in_=bias_ps[:, 0, :])
 
-        w_grp = const.tile([P, P, 4], BF16, name="w_grp", align_bytes=64)
-        nc.vector.tensor_copy(out=w_grp[:], in_=w_raw[:].rearrange("p t c -> p c t"))
-        w_codes = const.tile([P, P], U32, name="w_codes", align_bytes=64)
-        w_scales = const.tile([P, P], U8, name="w_scales", align_bytes=64)
-        nc.vector.quantize_mx(
-            out=w_codes[:].bitcast(FP8X4),
-            scales=w_scales[:],
-            in_=w_grp[:].rearrange("p c t -> p (c t)"),
-        )
+        def quantise_weights():
+            nc.vector.tensor_copy(out=w_grp[:], in_=w_raw[:].rearrange("p t c -> p c t"))
+            nc.vector.quantize_mx(
+                out=w_codes[:].bitcast(FP8X4),
+                scales=w_scales[:],
+                in_=w_grp[:].rearrange("p c t -> p (c t)"),
+            )
 
         def grp_of(t, half):
             key = ("grp", t, half)
             if key not in state:
-                if t % 4 == 0:
-                    state[key] = grp0_pool.tile([P, 2048], BF16, name="grp0", align_bytes=64)
+                if t % 4 == 3:
+                    state[key] = edge_pool.tile([P, 2048], BF16, name="edge", align_bytes=64)
                 else:
                     state[key] = grp_pool.tile([P, 2048], BF16, name="grp", align_bytes=64)
-            return state[key]
+            return state[key][:].bitcast(F32).rearrange("p (j m h) -> p j m h", j=4, h=2)
 
-        def transpose_and_exit(u):
-            c, half = u // 2, u % 2
+        def transpose_and_exit(c, half):
             a32 = attn_tiles[c][:].bitcast(F32)
-            t_next = (c // 4) * 4 + (c + 1) % 4
-            own32 = grp_of(c, half)[:].bitcast(F32).rearrange("p (j m h) -> p j m h", j=4, h=2)
-            next32 = grp_of(t_next, half)[:].bitcast(F32).rearrange("p (j m h) -> p j m h", j=4, h=2)
             banks = []
             for b in range(2):
                 tp = tp_pool.tile([P, 2, 2, P], F32, name="tp")
@@ -142,8 +148,13 @@ def tile_windowattentionblock_pb_t_kernel(tc, attn_ctx, x, wo, bo, out):
                 banks.append(tp)
             for b in range(2):
                 src = banks[b][:].rearrange("p a h m -> p a m h")
-                nc.scalar.copy(out=own32[:, 2 * b : 2 * b + 2, P - OWN : P, :], in_=src[:, :, 0:OWN, :])
-                nc.scalar.copy(out=next32[:, 2 * b : 2 * b + 2, 0 : P - OWN, :], in_=src[:, :, OWN:P, :])
+                js = slice(2 * b, 2 * b + 2)
+                if c % 4 == 3:
+                    own, prev = grp_of(c, half), grp_of((c - 4) % N_CHUNKS, half)
+                    nc.scalar.copy(out=own[:, js, 0:LAST_ROWS, :], in_=src[:, :, 0:LAST_ROWS, :])
+                    nc.scalar.copy(out=prev[:, js, LAST_ROWS:P, :], in_=src[:, :, LAST_ROWS:P, :])
+                else:
+                    nc.scalar.copy(out=grp_of(c, half)[:, js, :, :], in_=src)
 
         def quantise(t, half):
             codes = code_pool.tile([P, 512], U32, name="codes", align_bytes=64)
@@ -178,7 +189,7 @@ def tile_windowattentionblock_pb_t_kernel(tc, attn_ctx, x, wo, bo, out):
                 state[("o", t)] = out_pool.tile([P, 1024], F32, name="o_sb")
             nc.vector.tensor_tensor(
                 out=state[("o", t)][:, o_half(half)].rearrange("p (r c) -> p r c", r=4),
-                in0=x_tiles[t // 4][:, t % 4, o_half(half)].rearrange("p (r c) -> p r c", r=4),
+                in0=x_sb[:, t, o_half(half)].rearrange("p (r c) -> p r c", r=4),
                 in1=bias_bc[:].unsqueeze(1).to_broadcast([P, 4, P]),
                 op=ADD,
             )
@@ -191,36 +202,48 @@ def tile_windowattentionblock_pb_t_kernel(tc, attn_ctx, x, wo, bo, out):
                 in1=o_part,
                 op=ADD,
             )
-            if half == 1:
-                nc.sync.dma_start(out=out_v[t * P : (t + 1) * P, :], in_=state[("o", t)][:])
 
-        def complete_after(u):
-            c, half = u // 2, u % 2
-            done = []
-            if c % 4 != 0:
-                done.append((c, half))
-            elif c > 0:
-                done.append((c - 4, half))
-            if c == N_CHUNKS - 1:
-                done.append((c - 3, half))
-            return done
+        def store(t, cols=slice(0, 1024)):
+            for p0, p1, row in slots(t):
+                nc.sync.dma_start(out=out_v[row : row + p1 - p0, cols], in_=state[("o", t)][p0:p1, cols])
 
-        for s in range(N_UNITS + 3):
-            if s < N_UNITS:
-                transpose_and_exit(s)
-            if s == 1:
-                spread_bias()
-            if 0 <= s - 1 < N_UNITS:
-                for t, half in complete_after(s - 1):
-                    quantise(t, half)
-                    add_bias(t, half)
-            if 0 <= s - 2 < N_UNITS:
-                for t, half in complete_after(s - 2):
-                    multiply(t, half)
-            if s < N_UNITS and s % 2 == 1:
-                c_next = s // 2 + ATTN_BUFS
-                if c_next < N_CHUNKS:
-                    load_chunk(c_next)
-            if 0 <= s - 3 < N_UNITS:
-                for t, half in complete_after(s - 3):
-                    add_product(t, half)
+        def completed_by(i):
+            c = ORDER[i]
+            if c % 4 != 3:
+                return [c]
+            done = [] if c == 3 else [c - 4]
+            return done + [c] if c == N_CHUNKS - 1 else done
+
+        bias_order = [t for i in range(N_CHUNKS) for t in completed_by(i)]
+
+        for i in range(N_CHUNKS + 1):
+            if i < N_CHUNKS:
+                transpose_and_exit(ORDER[i], 0)
+                if i == 0:
+                    spread_bias()
+                    quantise_weights()
+                    add_bias(bias_order[0], 0)
+                    add_bias(bias_order[0], 1)
+                transpose_and_exit(ORDER[i], 1)
+            if i > 0:
+                for t in completed_by(i - 1):
+                    for half in range(2):
+                        multiply(t, half)
+            if i < N_CHUNKS:
+                for t in completed_by(i):
+                    quantise(t, 0)
+                for half in range(2):
+                    if i + 1 < N_CHUNKS:
+                        add_bias(bias_order[i + 1], half)
+                    if half == 0:
+                        for t in completed_by(i):
+                            quantise(t, 1)
+                if i + ATTN_BUFS < N_CHUNKS:
+                    load_step(i + ATTN_BUFS)
+            if i > 0:
+                for t in completed_by(i - 1):
+                    add_product(t, 0)
+                    if i == N_CHUNKS:
+                        store(t, o_half(0))
+                    add_product(t, 1)
+                    store(t, o_half(1) if i == N_CHUNKS else slice(0, 1024))

@@ -17,6 +17,8 @@ N_CHUNKS = 16
 ATTN_BUFS = 6
 OUT_BUFS = 16
 LAST_ROWS = 96
+WRAP = P - LAST_ROWS
+LAST = N_CHUNKS - 1
 
 ORDER = (
     [c for c in range(N_CHUNKS // 2) if c % 4 != 3]
@@ -51,31 +53,27 @@ def tile_windowattentionblock_pb_t_kernel(tc, attn_ctx, x, wo, bo, out):
         brow = const.tile([P, 256], BF16, name="brow")
         ones = const.tile([P, P], BF16, name="ones")
 
-        def slots(t):
-            if t < N_CHUNKS - 1:
-                return [(0, P, t * P + 32)]
-            return [(0, LAST_ROWS, t * P + 32), (LAST_ROWS, P, 0)]
+        def first_slot(t):
+            return t * P + WRAP if t < LAST else t * P
 
         def load_x(t0, t1):
-            if t1 <= N_CHUNKS - 1:
-                nc.sync.dma_start(
-                    out=x_sb[:, t0:t1, :],
-                    in_=x_v[t0 * P + 32 : t1 * P + 32, :].rearrange("(t q) f -> q t f", q=P),
-                )
-            else:
-                for p0, p1, row in slots(t0):
-                    nc.sync.dma_start(out=x_sb[p0:p1, t0, :], in_=x_v[row : row + p1 - p0, :])
+            nc.sync.dma_start(
+                out=x_sb[:, t0:t1, :],
+                in_=x_v[first_slot(t0) : first_slot(t0) + (t1 - t0) * P, :].rearrange("(t q) f -> q t f", q=P),
+            )
 
         def load_attn(c, lo=0, hi=4096):
             if c not in attn_tiles:
                 attn_tiles[c] = attn_pool.tile([P, 4096], BF16, name="a_sb")
             nc.sync.dma_start(out=attn_tiles[c][:, lo:hi], in_=attn_v[c * P : (c + 1) * P, lo:hi])
 
-        x_before = {1: (1, 3), 2: (3, 7), 4: (7, 12), 7: (12, 15), 8: (15, 16)}
+        x_before = {1: (1, 3), 2: (3, 7), 4: (7, 12), 5: (LAST, LAST + 1), 7: (12, LAST)}
 
         def load_step(i):
             if i in x_before:
                 load_x(*x_before[i])
+            if i == 8:
+                nc.sync.dma_start(out=x_sb[0:WRAP, LAST, :], in_=x_v[0:WRAP, :])
             load_attn(ORDER[i])
 
         nc.vector.memset(brow[:], 0.0)
@@ -151,8 +149,10 @@ def tile_windowattentionblock_pb_t_kernel(tc, attn_ctx, x, wo, bo, out):
                 js = slice(2 * b, 2 * b + 2)
                 if c % 4 == 3:
                     own, prev = grp_of(c, half), grp_of((c - 4) % N_CHUNKS, half)
-                    nc.scalar.copy(out=own[:, js, 0:LAST_ROWS, :], in_=src[:, :, 0:LAST_ROWS, :])
-                    nc.scalar.copy(out=prev[:, js, LAST_ROWS:P, :], in_=src[:, :, LAST_ROWS:P, :])
+                    own_cols = slice(WRAP, P) if c == LAST else slice(0, LAST_ROWS)
+                    prev_cols = slice(0, WRAP) if c == 3 else slice(LAST_ROWS, P)
+                    nc.scalar.copy(out=own[:, js, own_cols, :], in_=src[:, :, 0:LAST_ROWS, :])
+                    nc.scalar.copy(out=prev[:, js, prev_cols, :], in_=src[:, :, LAST_ROWS:P, :])
                 else:
                     nc.scalar.copy(out=grp_of(c, half)[:, js, :, :], in_=src)
 
@@ -204,8 +204,10 @@ def tile_windowattentionblock_pb_t_kernel(tc, attn_ctx, x, wo, bo, out):
             )
 
         def store(t, cols=slice(0, 1024)):
-            for p0, p1, row in slots(t):
-                nc.sync.dma_start(out=out_v[row : row + p1 - p0, cols], in_=state[("o", t)][p0:p1, cols])
+            row = first_slot(t)
+            nc.sync.dma_start(out=out_v[row : row + P, cols], in_=state[("o", t)][:, cols])
+            if t == LAST:
+                nc.sync.dma_start(out=out_v[0:WRAP, cols], in_=state[("o", t)][0:WRAP, cols])
 
         def completed_by(i):
             c = ORDER[i]

@@ -14,7 +14,7 @@ P = 128
 FLOPS = 2 * 16384 * 512 * 128
 
 N_CHUNKS = 16
-ATTN_BUFS = 6
+ATTN_BUFS = 7
 OUT_BUFS = 16
 LAST_ROWS = 96
 WRAP = P - LAST_ROWS
@@ -56,25 +56,32 @@ def tile_windowattentionblock_pb_t_kernel(tc, attn_ctx, x, wo, bo, out):
         def first_slot(t):
             return t * P + WRAP if t < LAST else t * P
 
-        def load_x(t0, t1):
-            nc.sync.dma_start(
-                out=x_sb[:, t0:t1, :],
-                in_=x_v[first_slot(t0) : first_slot(t0) + (t1 - t0) * P, :].rearrange("(t q) f -> q t f", q=P),
-            )
+        def load_x(t):
+            nc.sync.dma_start(out=x_sb[:, t, :], in_=x_v[first_slot(t) : first_slot(t) + P, :])
 
         def load_attn(c, lo=0, hi=4096):
             if c not in attn_tiles:
                 attn_tiles[c] = attn_pool.tile([P, 4096], BF16, name="a_sb")
             nc.sync.dma_start(out=attn_tiles[c][:, lo:hi], in_=attn_v[c * P : (c + 1) * P, lo:hi])
 
-        x_before = {1: (1, 3), 2: (3, 7), 4: (7, 12), 5: (LAST, LAST + 1), 7: (12, LAST)}
-
         def load_step(i):
-            if i in x_before:
-                load_x(*x_before[i])
-            if i == 8:
-                nc.sync.dma_start(out=x_sb[0:WRAP, LAST, :], in_=x_v[0:WRAP, :])
             load_attn(ORDER[i])
+            for j in range(0 if i == 1 else i, i + 1):
+                if bias_order[j] == LAST:
+                    nc.sync.dma_start(out=x_sb[0:WRAP, LAST, :], in_=x_v[0:WRAP, :])
+                else:
+                    load_x(bias_order[j])
+            if i == 5:
+                load_x(LAST)
+
+        def completed_by(i):
+            c = ORDER[i]
+            if c % 4 != 3:
+                return [c]
+            done = [] if c == 3 else [c - 4]
+            return done + [c] if c == N_CHUNKS - 1 else done
+
+        bias_order = [t for i in range(N_CHUNKS) for t in completed_by(i)]
 
         nc.vector.memset(brow[:], 0.0)
         nc.vector.memset(ones[:], 1.0)
@@ -82,7 +89,6 @@ def tile_windowattentionblock_pb_t_kernel(tc, attn_ctx, x, wo, bo, out):
         nc.sync.dma_start(out=brow[0:1, 0:P], in_=bo.unsqueeze(0))
         load_attn(ORDER[0], 1024, 2048)
         nc.sync.dma_start(out=w_raw[:].rearrange("p t c -> p (t c)"), in_=wo_v)
-        load_x(0, 1)
         load_attn(ORDER[0], 2048, 4096)
         for i in range(1, ATTN_BUFS):
             load_step(i)
@@ -203,20 +209,11 @@ def tile_windowattentionblock_pb_t_kernel(tc, attn_ctx, x, wo, bo, out):
                 op=ADD,
             )
 
-        def store(t, cols=slice(0, 1024)):
+        def store(t):
             row = first_slot(t)
-            nc.sync.dma_start(out=out_v[row : row + P, cols], in_=state[("o", t)][:, cols])
+            nc.sync.dma_start(out=out_v[row : row + P, :], in_=state[("o", t)][:])
             if t == LAST:
-                nc.sync.dma_start(out=out_v[0:WRAP, cols], in_=state[("o", t)][0:WRAP, cols])
-
-        def completed_by(i):
-            c = ORDER[i]
-            if c % 4 != 3:
-                return [c]
-            done = [] if c == 3 else [c - 4]
-            return done + [c] if c == N_CHUNKS - 1 else done
-
-        bias_order = [t for i in range(N_CHUNKS) for t in completed_by(i)]
+                nc.sync.dma_start(out=out_v[0:WRAP, :], in_=state[("o", t)][0:WRAP, :])
 
         for i in range(N_CHUNKS + 1):
             if i < N_CHUNKS:
@@ -245,7 +242,5 @@ def tile_windowattentionblock_pb_t_kernel(tc, attn_ctx, x, wo, bo, out):
             if i > 0:
                 for t in completed_by(i - 1):
                     add_product(t, 0)
-                    if i == N_CHUNKS:
-                        store(t, o_half(0))
                     add_product(t, 1)
-                    store(t, o_half(1) if i == N_CHUNKS else slice(0, 1024))
+                    store(t)

@@ -15,10 +15,12 @@ FLOPS = 2 * 16384 * 512 * 128
 
 N_CHUNKS = 16
 ATTN_BUFS = 7
-OUT_BUFS = 16
 LAST_ROWS = 96
 WRAP = P - LAST_ROWS
 LAST = N_CHUNKS - 1
+
+X_BEHIND = {1: [(0, 3)], 3: [(3, 8)], 6: [(LAST, LAST + 1)], 7: [(8, 12)], 11: [(12, LAST)]}
+STORES = {2: (0, 3), 3: (3, 4), 6: (4, 7), 7: (7, 8), 10: (8, 11)} | {t: (t, t + 1) for t in range(11, N_CHUNKS)}
 
 ORDER = (
     [c for c in range(N_CHUNKS // 2) if c % 4 != 3]
@@ -40,7 +42,6 @@ def tile_windowattentionblock_pb_t_kernel(tc, attn_ctx, x, wo, bo, out):
         grp_pool = ctx.enter_context(tc.tile_pool(name="grp", bufs=6))
         edge_pool = ctx.enter_context(tc.tile_pool(name="edge", bufs=8))
         code_pool = ctx.enter_context(tc.tile_pool(name="code", bufs=5))
-        out_pool = ctx.enter_context(tc.tile_pool(name="outp", bufs=OUT_BUFS))
         tp_pool = ctx.enter_context(tc.psum_pool(name="tp", bufs=4))
         mx_pool = ctx.enter_context(tc.psum_pool(name="mx", bufs=4))
         ctx.enter_context(tc.manual_schedule())
@@ -48,6 +49,7 @@ def tile_windowattentionblock_pb_t_kernel(tc, attn_ctx, x, wo, bo, out):
         attn_tiles = {}
         state = {}
 
+        o_all = const.tile([P, N_CHUNKS, 1024], F32, name="o_all")
         x_sb = const.tile([P, N_CHUNKS, 1024], BF16, name="x_sb")
         w_raw = const.tile([P, 4, P], BF16, name="w_raw")
         brow = const.tile([P, 256], BF16, name="brow")
@@ -56,8 +58,11 @@ def tile_windowattentionblock_pb_t_kernel(tc, attn_ctx, x, wo, bo, out):
         def first_slot(t):
             return t * P + WRAP if t < LAST else t * P
 
-        def load_x(t):
-            nc.sync.dma_start(out=x_sb[:, t, :], in_=x_v[first_slot(t) : first_slot(t) + P, :])
+        def load_x(t0, t1):
+            nc.sync.dma_start(
+                out=x_sb[:, t0:t1, :],
+                in_=x_v[first_slot(t0) : first_slot(t0) + (t1 - t0) * P, :].rearrange("(t q) f -> q t f", q=P),
+            )
 
         def load_attn(c, lo=0, hi=4096):
             if c not in attn_tiles:
@@ -66,13 +71,10 @@ def tile_windowattentionblock_pb_t_kernel(tc, attn_ctx, x, wo, bo, out):
 
         def load_step(i):
             load_attn(ORDER[i])
-            for j in range(0 if i == 1 else i, i + 1):
-                if bias_order[j] == LAST:
-                    nc.sync.dma_start(out=x_sb[0:WRAP, LAST, :], in_=x_v[0:WRAP, :])
-                else:
-                    load_x(bias_order[j])
-            if i == 5:
-                load_x(LAST)
+            for t0, t1 in X_BEHIND.get(i, ()):
+                load_x(t0, t1)
+            if i == 9:
+                nc.sync.dma_start(out=x_sb[0:WRAP, LAST, :], in_=x_v[0:WRAP, :])
 
         def completed_by(i):
             c = ORDER[i]
@@ -191,17 +193,15 @@ def tile_windowattentionblock_pb_t_kernel(tc, attn_ctx, x, wo, bo, out):
             return slice(lo, lo + 512)
 
         def add_bias(t, half):
-            if half == 0:
-                state[("o", t)] = out_pool.tile([P, 1024], F32, name="o_sb")
             nc.vector.tensor_tensor(
-                out=state[("o", t)][:, o_half(half)].rearrange("p (r c) -> p r c", r=4),
+                out=o_all[:, t, o_half(half)].rearrange("p (r c) -> p r c", r=4),
                 in0=x_sb[:, t, o_half(half)].rearrange("p (r c) -> p r c", r=4),
                 in1=bias_bc[:].unsqueeze(1).to_broadcast([P, 4, P]),
                 op=ADD,
             )
 
         def add_product(t, half):
-            o_part = state[("o", t)][:, o_half(half)]
+            o_part = o_all[:, t, o_half(half)]
             nc.vector.tensor_tensor(
                 out=o_part,
                 in0=state[("mx", t, half)][:].rearrange("p a c -> p (a c)"),
@@ -209,11 +209,13 @@ def tile_windowattentionblock_pb_t_kernel(tc, attn_ctx, x, wo, bo, out):
                 op=ADD,
             )
 
-        def store(t):
-            row = first_slot(t)
-            nc.sync.dma_start(out=out_v[row : row + P, :], in_=state[("o", t)][:])
-            if t == LAST:
-                nc.sync.dma_start(out=out_v[0:WRAP, :], in_=state[("o", t)][0:WRAP, :])
+        def store(t0, t1):
+            nc.sync.dma_start(
+                out=out_v[first_slot(t0) : first_slot(t0) + (t1 - t0) * P, :].rearrange("(t q) f -> q t f", q=P),
+                in_=o_all[:, t0:t1, :],
+            )
+            if t0 == LAST:
+                nc.sync.dma_start(out=out_v[0:WRAP, :], in_=o_all[0:WRAP, LAST, :])
 
         for i in range(N_CHUNKS + 1):
             if i < N_CHUNKS:
@@ -243,4 +245,5 @@ def tile_windowattentionblock_pb_t_kernel(tc, attn_ctx, x, wo, bo, out):
                 for t in completed_by(i - 1):
                     add_product(t, 0)
                     add_product(t, 1)
-                    store(t)
+                    if t in STORES:
+                        store(*STORES[t])

from contextlib import ExitStack

import concourse.mybir as mybir
from concourse.masks import make_identity

F32 = mybir.dt.float32
BF16 = mybir.dt.bfloat16
U32 = mybir.dt.uint32
U8 = mybir.dt.uint8
FP8X4 = mybir.dt.float8_e4m3fn_x4
ADD = mybir.AluOpType.add

P = 128
FLOPS = 2 * 16384 * 512 * 128

N_CHUNKS = 16
ATTN_BUFS = 7
LAST_ROWS = 96
WRAP = P - LAST_ROWS
LAST = N_CHUNKS - 1

X_BEHIND = {1: [(0, 3)], 3: [(3, 8)], 6: [(LAST, LAST + 1)], 7: [(8, 12)], 11: [(12, LAST)]}
STORES = {2: (0, 3), 3: (3, 4), 6: (4, 7), 7: (7, 8), 10: (8, 11)} | {t: (t, t + 1) for t in range(11, N_CHUNKS)}

ORDER = (
    [c for c in range(N_CHUNKS // 2) if c % 4 != 3]
    + [c for c in range(N_CHUNKS) if c % 4 == 3]
    + [c for c in range(N_CHUNKS // 2, N_CHUNKS) if c % 4 != 3]
)


def tile_windowattentionblock_pb_t_kernel(tc, attn_ctx, x, wo, bo, out):
    nc = tc.nc
    attn_v = attn_ctx.rearrange("n (ti tj) h d -> (n ti) (tj h d)", tj=8)
    x_v = x.rearrange("b i (s r) c -> (b i s) (r c)", r=8)
    out_v = out.rearrange("b i (s r) c -> (b i s) (r c)", r=8)
    wo_v = wo.rearrange("h d c -> (h d) c").rearrange("(q t) c -> q (t c)", t=4)

    with ExitStack() as ctx:
        const = ctx.enter_context(tc.tile_pool(name="const", bufs=1))
        attn_pool = ctx.enter_context(tc.tile_pool(name="attn", bufs=ATTN_BUFS))
        grp_pool = ctx.enter_context(tc.tile_pool(name="grp", bufs=6))
        edge_pool = ctx.enter_context(tc.tile_pool(name="edge", bufs=8))
        code_pool = ctx.enter_context(tc.tile_pool(name="code", bufs=5))
        tp_pool = ctx.enter_context(tc.psum_pool(name="tp", bufs=4))
        mx_pool = ctx.enter_context(tc.psum_pool(name="mx", bufs=4))
        ctx.enter_context(tc.manual_schedule())

        attn_tiles = {}
        state = {}

        o_all = const.tile([P, N_CHUNKS, 1024], F32, name="o_all")
        x_sb = const.tile([P, N_CHUNKS, 1024], BF16, name="x_sb")
        w_raw = const.tile([P, 4, P], BF16, name="w_raw")
        brow = const.tile([P, 256], BF16, name="brow")
        ones = const.tile([P, P], BF16, name="ones")

        def first_slot(t):
            return t * P + WRAP if t < LAST else t * P

        def load_x(t0, t1):
            nc.sync.dma_start(
                out=x_sb[:, t0:t1, :],
                in_=x_v[first_slot(t0) : first_slot(t0) + (t1 - t0) * P, :].rearrange("(t q) f -> q t f", q=P),
            )

        def load_attn(c, lo=0, hi=4096):
            if c not in attn_tiles:
                attn_tiles[c] = attn_pool.tile([P, 4096], BF16, name="a_sb")
            nc.sync.dma_start(out=attn_tiles[c][:, lo:hi], in_=attn_v[c * P : (c + 1) * P, lo:hi])

        def load_step(i):
            load_attn(ORDER[i])
            for t0, t1 in X_BEHIND.get(i, ()):
                load_x(t0, t1)
            if i == 9:
                nc.sync.dma_start(out=x_sb[0:WRAP, LAST, :], in_=x_v[0:WRAP, :])

        def completed_by(i):
            c = ORDER[i]
            if c % 4 != 3:
                return [c]
            done = [] if c == 3 else [c - 4]
            return done + [c] if c == N_CHUNKS - 1 else done

        bias_order = [t for i in range(N_CHUNKS) for t in completed_by(i)]

        nc.vector.memset(brow[:], 0.0)
        nc.vector.memset(ones[:], 1.0)
        load_attn(ORDER[0], 0, 1024)
        nc.sync.dma_start(out=brow[0:1, 0:P], in_=bo.unsqueeze(0))
        load_attn(ORDER[0], 1024, 2048)
        nc.sync.dma_start(out=w_raw[:].rearrange("p t c -> p (t c)"), in_=wo_v)
        load_attn(ORDER[0], 2048, 4096)
        for i in range(1, ATTN_BUFS):
            load_step(i)

        ident = const.tile([P, P], F32, name="ident")
        make_identity(nc, ident[:])
        id_v = ident[:].rearrange("p (g j t) -> p g t j", g=2, j=8)
        perm_a = const.tile([P, 2, 8, 8], F32, name="perm_a")
        perm_b = const.tile([P, 2, 8, 8], F32, name="perm_b")
        nc.vector.tensor_copy(out=perm_a[:], in_=id_v)
        nc.vector.tensor_copy(out=perm_b[:, :, :, 1:8], in_=id_v[:, :, :, 0:7])
        nc.vector.tensor_copy(out=perm_b[:, :, :, 0:1], in_=id_v[:, :, :, 7:8])
        perms = [
            perm_a[:].rearrange("p g t s -> p (g t s)"),
            perm_b[:].rearrange("p g t s -> p (g t s)"),
        ]

        bias_bc = const.tile([P, P], F32, name="bias_bc")
        w_grp = const.tile([P, P, 4], BF16, name="w_grp", align_bytes=64)
        w_codes = const.tile([P, P], U32, name="w_codes", align_bytes=64)
        w_scales = const.tile([P, P], U8, name="w_scales", align_bytes=64)

        def spread_bias():
            bias_ps = mx_pool.tile([P, 4, P], F32, name="bias_ps", tag="mx")
            nc.tensor.matmul(
                out=bias_ps[:, 0:2, :].rearrange("p a c -> p (a c)"),
                lhsT=ones[:],
                rhs=brow[:],
                start=True,
                stop=True,
            )
            nc.vector.tensor_copy(out=bias_bc[:], in_=bias_ps[:, 0, :])

        def quantise_weights():
            nc.vector.tensor_copy(out=w_grp[:], in_=w_raw[:].rearrange("p t c -> p c t"))
            nc.vector.quantize_mx(
                out=w_codes[:].bitcast(FP8X4),
                scales=w_scales[:],
                in_=w_grp[:].rearrange("p c t -> p (c t)"),
            )

        def grp_of(t, half):
            key = ("grp", t, half)
            if key not in state:
                if t % 4 == 3:
                    state[key] = edge_pool.tile([P, 2048], BF16, name="edge", align_bytes=64)
                else:
                    state[key] = grp_pool.tile([P, 2048], BF16, name="grp", align_bytes=64)
            return state[key][:].bitcast(F32).rearrange("p (j m h) -> p j m h", j=4, h=2)

        def transpose_and_exit(c, half):
            a32 = attn_tiles[c][:].bitcast(F32)
            banks = []
            for b in range(2):
                tp = tp_pool.tile([P, 2, 2, P], F32, name="tp")
                for a in range(2):
                    tj = half * 4 + b * 2 + a
                    for h in range(2):
                        words = slice(tj * 256 + h, (tj + 1) * 256, 2)
                        nc.tensor.transpose(tp[:, a, h, :], a32[:, words], perms[half])
                banks.append(tp)
            for b in range(2):
                src = banks[b][:].rearrange("p a h m -> p a m h")
                js = slice(2 * b, 2 * b + 2)
                if c % 4 == 3:
                    own, prev = grp_of(c, half), grp_of((c - 4) % N_CHUNKS, half)
                    own_cols = slice(WRAP, P) if c == LAST else slice(0, LAST_ROWS)
                    prev_cols = slice(0, WRAP) if c == 3 else slice(LAST_ROWS, P)
                    nc.scalar.copy(out=own[:, js, own_cols, :], in_=src[:, :, 0:LAST_ROWS, :])
                    nc.scalar.copy(out=prev[:, js, prev_cols, :], in_=src[:, :, LAST_ROWS:P, :])
                else:
                    nc.scalar.copy(out=grp_of(c, half)[:, js, :, :], in_=src)

        def quantise(t, half):
            codes = code_pool.tile([P, 512], U32, name="codes", align_bytes=64)
            scales = code_pool.tile([P, 512], U8, name="scales", align_bytes=64)
            nc.vector.quantize_mx(
                out=codes[:].bitcast(FP8X4), scales=scales[:], in_=state[("grp", t, half)][:]
            )
            state[("codes", t, half)] = (codes, scales)

        def multiply(t, half):
            codes, scales = state[("codes", t, half)]
            mx = mx_pool.tile([P, 4, P], F32, name="mx")
            for a in range(4):
                cols = slice(a * P, (a + 1) * P)
                nc.tensor.matmul_mx(
                    out=mx[:, a, :],
                    lhsT=codes[:, cols].bitcast(FP8X4),
                    lhsT_scale=scales[:, cols],
                    rhs=w_codes[:].bitcast(FP8X4),
                    rhs_scale=w_scales[:],
                    start=True,
                    stop=True,
                )
            state[("mx", t, half)] = mx

        def o_half(half):
            lo = 512 if half == 0 else 0
            return slice(lo, lo + 512)

        def add_bias(t, half):
            nc.vector.tensor_tensor(
                out=o_all[:, t, o_half(half)].rearrange("p (r c) -> p r c", r=4),
                in0=x_sb[:, t, o_half(half)].rearrange("p (r c) -> p r c", r=4),
                in1=bias_bc[:].unsqueeze(1).to_broadcast([P, 4, P]),
                op=ADD,
            )

        def add_product(t, half):
            o_part = o_all[:, t, o_half(half)]
            nc.vector.tensor_tensor(
                out=o_part,
                in0=state[("mx", t, half)][:].rearrange("p a c -> p (a c)"),
                in1=o_part,
                op=ADD,
            )

        def store(t0, t1):
            nc.sync.dma_start(
                out=out_v[first_slot(t0) : first_slot(t0) + (t1 - t0) * P, :].rearrange("(t q) f -> q t f", q=P),
                in_=o_all[:, t0:t1, :],
            )
            if t0 == LAST:
                nc.sync.dma_start(out=out_v[0:WRAP, :], in_=o_all[0:WRAP, LAST, :])

        for i in range(N_CHUNKS + 1):
            if i < N_CHUNKS:
                transpose_and_exit(ORDER[i], 0)
                if i == 0:
                    spread_bias()
                    quantise_weights()
                    add_bias(bias_order[0], 0)
                    add_bias(bias_order[0], 1)
                transpose_and_exit(ORDER[i], 1)
            if i > 0:
                for t in completed_by(i - 1):
                    for half in range(2):
                        multiply(t, half)
            if i < N_CHUNKS:
                for t in completed_by(i):
                    quantise(t, 0)
                for half in range(2):
                    if i + 1 < N_CHUNKS:
                        add_bias(bias_order[i + 1], half)
                    if half == 0:
                        for t in completed_by(i):
                            quantise(t, 1)
                if i + ATTN_BUFS < N_CHUNKS:
                    load_step(i + ATTN_BUFS)
            if i > 0:
                for t in completed_by(i - 1):
                    add_product(t, 0)
                    add_product(t, 1)
                    if t in STORES:
                        store(*STORES[t])
